import numpy as np
import ml_dtypes


def mxq(x, axis, fmt="e4m3"):
    dtype, down = {"e4m3": (ml_dtypes.float8_e4m3fn, 7), "e5m2": (ml_dtypes.float8_e5m2, 14)}[fmt]
    v = np.moveaxis(np.asarray(x, np.float32).astype(ml_dtypes.bfloat16).astype(np.float64), axis, -1)
    blocks = v.reshape(v.shape[:-1] + (-1, 32))
    amax = np.abs(blocks).max(-1, keepdims=True)
    byte = np.maximum(np.where(amax > 0, np.frexp(amax)[1] - 1 + 127, 0) - down, 1)
    scale = np.exp2(byte - 127.0)
    codes = (blocks / scale).astype(np.float32).astype(dtype).astype(np.float64)
    return np.moveaxis((codes * scale).reshape(v.shape), -1, axis)


WIDE = False


def mx_kscale(k):
    if not WIDE:
        return np.ones(k)
    levels = np.array([10, -10, 5, -5, 0])
    if k % 512:
        return np.exp2(np.random.permutation(np.resize(levels, k // 32))).repeat(32)
    a = np.empty((k // 512, 16))
    for p in range(k // 512):
        a[p, :8] = np.random.permutation(np.resize(levels, 8))
        for g in range(8):
            far = levels[np.abs(levels - a[p, g]) >= 10]
            a[p, g + 8] = far[np.random.randint(len(far))]
    return np.exp2(a.ravel()).repeat(32)


BF16 = ml_dtypes.bfloat16


def bf(x):
    return np.asarray(x, np.float32).astype(BF16)


def f64(x):
    return np.asarray(x).astype(np.float64)


N, F, H = 1536, 512, 512
SIG = 1.5


def draw_adj():
    r = np.random.uniform(0.5, 1.5, (N, 1))
    return 2.0 * r * np.exp(SIG * np.random.standard_normal((N, N)) - 0.5 * SIG * SIG) / N


def draw0():
    s, t = mx_kscale(F), mx_kscale(N)
    return {"x_init": bf(np.random.standard_normal((N, F)) * s / t[:, None]),
            "adj1": bf(draw_adj() * t),
            "W1": bf(np.random.standard_normal((F, H)) * 4.0 / np.sqrt(F) / s[:, None]),
            "b1": bf(np.random.standard_normal(H) * 0.3)}


def core(x_init, adj1, W1, b1):
    support = mxq(f64(x_init), 1, "e4m3") @ mxq(f64(W1), 0, "e4m3")
    y = (mxq(f64(adj1), 1, "e4m3") @ mxq(support, 0, "e4m3")) + f64(b1)
    return np.maximum(y, 0.0)


def e4m3fn_bytes(y):
    return np.clip(np.asarray(y, np.float64), -448.0, 448.0).astype(np.float32).astype(ml_dtypes.float8_e4m3fn).view(np.uint8)


def e4m3fn_values(b):
    return np.asarray(b, np.uint8).view(ml_dtypes.float8_e4m3fn).astype(np.float64)


def setup_inputs():
    d = draw0()
    x0 = np.asarray(d['adj1']).astype(np.float64)
    s = (np.max(np.abs(x0), axis=(0,), keepdims=True) / 448.0).astype(np.float32)
    out = {}
    for k, v in d.items():
        if k == 'adj1':
            out['adj1_bytes'] = e4m3fn_bytes(x0 / s.astype(np.float64))
            out['adj1_scale'] = s
        else:
            out[k] = v
    return out


def reference(x_init, adj1_bytes, adj1_scale, W1, b1):
    return core(x_init, e4m3fn_values(adj1_bytes) * adj1_scale.astype(np.float64), W1, b1)

@@ -1,0 +1,297 @@
+from contextlib import ExitStack
+
+import concourse.mybir as mybir
+from concourse.masks import make_identity
+
+N, F, H = 1536, 512, 512
+FLOPS = 2 * N * F * H + 2 * N * N * H
+
+F32 = mybir.dt.float32
+BF16 = mybir.dt.bfloat16
+U32 = mybir.dt.uint32
+U8 = mybir.dt.uint8
+FP8 = mybir.dt.float8_e4m3fn
+FP8X4 = mybir.dt.float8_e4m3fn_x4
+ALU = mybir.AluOpType
+ACT = mybir.ActivationFunctionType
+
+P = 128
+PACK = 4
+K_PASS = P * PACK
+PASSES = N // K_PASS
+TILES = N // P
+
+
+def tile_gcn_pa_kernel(tc, x_init, adj1_bytes, adj1_scale, W1, b1, out):
+    nc = tc.nc
+    with ExitStack() as ctx:
+        keep = ctx.enter_context(tc.tile_pool(name="keep", bufs=1))
+        work = ctx.enter_context(tc.tile_pool(name="work", bufs=4))
+        turn_banks = ctx.enter_context(tc.psum_pool(name="turn_banks", bufs=4))
+        sum_banks = ctx.enter_context(tc.psum_pool(name="sum_banks", bufs=4))
+        ctx.enter_context(tc.manual_schedule())
+
+        def kept(name, width, dtype):
+            return keep.tile([P, width], dtype, name=name, align_bytes=64)
+
+        scale_cols = kept("scale_cols", PASSES * PACK, F32)
+        scale_rows = kept("scale_rows", N, F32)
+        bias_rows = kept("bias_rows", H, BF16)
+        ident = kept("ident", P, F32)
+        w_raw = kept("w_raw", PACK * H, BF16)
+        w_grouped = kept("w_grouped", H * PACK, BF16)
+        w_codes = kept("w_codes", H, U32)
+        w_scales = kept("w_scales", H, U8)
+        x_raw = [kept("x_raw%d" % g, PACK * F, BF16) for g in range(PASSES)]
+        x_grouped = [kept("x_grouped%d" % g, K_PASS * PACK, BF16) for g in range(PASSES)]
+        x_codes = [kept("x_codes%d" % g, K_PASS, U32) for g in range(PASSES)]
+        x_scales = [kept("x_scales%d" % g, K_PASS, U8) for g in range(PASSES)]
+        sup_grouped = [kept("sup_grouped%d" % g, H * PACK, BF16) for g in range(PASSES)]
+        sup_codes = [kept("sup_codes%d" % g, H, U32) for g in range(PASSES)]
+        sup_scales = [kept("sup_scales%d" % g, H, U8) for g in range(PASSES)]
+        adj_fp8 = [kept("adj_fp8_%d" % n, N, U8) for n in range(TILES)]
+        bank_passes = [(0, 1), (2,)]
+        adj_codes = [[kept("adj_codes%d_%d" % (n, b), P * len(gs), U32) for b, gs in enumerate(bank_passes)] for n in range(TILES)]
+        adj_scales = [[kept("adj_scales%d_%d" % (n, b), P * len(gs), U8) for b, gs in enumerate(bank_passes)] for n in range(TILES)]
+
+        adj_wide = {}
+        adj_turned = {}
+        adj_grouped = {}
+        x_turned = {}
+        sup_sums = {}
+        out_sums = {}
+
+        def load_adj(n):
+            nc.sync.dma_start(out=adj_fp8[n][:], in_=adj1_bytes[n * P : (n + 1) * P, :])
+
+        def load_x(g):
+            rows = x_init[g * K_PASS : (g + 1) * K_PASS, :]
+            nc.sync.dma_start(out=x_raw[g][:], in_=rows.rearrange("(m t) k -> m (t k)", t=PACK))
+
+        nc.scalar.dma_start(
+            out=scale_cols[:].rearrange("p (g t) -> p g t", t=PACK),
+            in_=adj1_scale.rearrange("o (g p t) -> p (o g) t", p=P, t=PACK),
+        )
+        nc.sync.dma_start(out=w_raw[:], in_=W1.rearrange("(p j) h -> p (j h)", j=PACK))
+        load_adj(0)
+        for g in range(PASSES):
+            load_adj(g + 1)
+            load_x(g)
+        for n in range(PASSES + 1, TILES):
+            load_adj(n)
+        nc.sync.dma_start(out=bias_rows[:], in_=b1.partition_broadcast(P))
+
+        make_identity(nc, ident[:])
+
+        def spread_scale(g):
+            bank = turn_banks.tile([P, PACK, P], F32, name="turn")
+            for t in range(PACK):
+                col = g * PACK + t
+                nc.tensor.transpose(bank[:, t, :], scale_cols[:, col : col + 1].to_broadcast([P, P]), ident[:])
+            rows = scale_rows[:, g * K_PASS : (g + 1) * K_PASS]
+            nc.scalar.copy(out=rows.rearrange("q (p t) -> q p t", t=PACK), in_=bank[:].rearrange("q t p -> q p t"))
+
+        def group_w(copy, half):
+            cols = H // 2
+            src = w_raw[:].rearrange("p (j h) -> p j h", j=PACK)[:, :, half * cols : (half + 1) * cols]
+            dst = w_grouped[:, half * cols * PACK : (half + 1) * cols * PACK]
+            copy(out=dst.rearrange("p (c i j) -> p c j i", i=4, j=PACK), in_=src.rearrange("p j (c i) -> p c j i", i=4))
+
+        def quantize(codes, scales, grouped):
+            nc.vector.quantize_mx(out=codes[:].bitcast(FP8X4), scales=scales[:], in_=grouped[:])
+
+        def turn_x(g):
+            words = x_raw[g][:].bitcast(F32)
+            for b in range(2):
+                bank = turn_banks.tile([P, 2, 2, P], F32, name="turn")
+                for tt in range(2):
+                    first = (2 * b + tt) * (F // 2)
+                    for u in range(2):
+                        nc.tensor.transpose(bank[:, tt, u, :], words[:, first + u : first + F // 2 : 2], ident[:])
+                x_turned[g, b] = bank
+
+        def group_x(g):
+            for b in range(2):
+                dst = x_grouped[g][:, b * 2 * K_PASS : (b + 1) * 2 * K_PASS].bitcast(F32)
+                nc.scalar.copy(
+                    out=dst.rearrange("p (t m u) -> p t m u", t=2, u=2),
+                    in_=x_turned[g, b][:].rearrange("p t u m -> p t m u"),
+                )
+
+        def multiply_support(g):
+            for c in range(H // P):
+                bank = sum_banks.tile([P, PACK, P], F32, name="sums")
+                cols = slice(c * P, (c + 1) * P)
+                for t in range(PACK):
+                    nodes = slice(t * P, (t + 1) * P)
+                    nc.tensor.matmul_mx(
+                        out=bank[:, t, :],
+                        lhsT=x_codes[g][:, nodes].bitcast(FP8X4),
+                        lhsT_scale=x_scales[g][:, nodes],
+                        rhs=w_codes[:, cols].bitcast(FP8X4),
+                        rhs_scale=w_scales[:, cols],
+                        start=True,
+                        stop=True,
+                    )
+                sup_sums[g, c] = bank
+
+        def group_support(g):
+            for c in range(H // P):
+                dst = sup_grouped[g][:, c * K_PASS : (c + 1) * K_PASS]
+                nc.scalar.copy(out=dst.rearrange("p (h t) -> p h t", t=PACK), in_=sup_sums[g, c][:].rearrange("p t h -> p h t"))
+
+        def widen_adj(n, pieces=1):
+            wide = work.tile([P, N], BF16, name="adj_wide", align_bytes=64)
+            width = N // pieces
+            for c in range(pieces):
+                cols = slice(c * width, (c + 1) * width)
+                nc.vector.tensor_tensor(out=wide[:, cols], in0=adj_fp8[n][:, cols].bitcast(FP8), in1=scale_rows[:, cols], op=ALU.mult)
+            adj_wide[n] = wide
+
+        def turn_adj(n):
+            words = adj_wide[n][:].bitcast(F32)
+            for b, gs in enumerate(bank_passes):
+                bank = turn_banks.tile([P, len(gs), 2, P], F32, name="turn")
+                for slot, g in enumerate(gs):
+                    first = g * (K_PASS // 2)
+                    for u in range(2):
+                        nc.tensor.transpose(bank[:, slot, u, :], words[:, first + u : first + K_PASS // 2 : 2], ident[:])
+                adj_turned[n, b] = bank
+
+        def group_adj(n):
+            for b, gs in enumerate(bank_passes):
+                grouped = work.tile([P, len(gs) * K_PASS], BF16, name="adj_grouped%d" % b, align_bytes=64)
+                nc.scalar.copy(
+                    out=grouped[:].bitcast(F32).rearrange("p (g r u) -> p g r u", g=len(gs), u=2),
+                    in_=adj_turned[n, b][:].rearrange("p g u r -> p g r u"),
+                )
+                adj_grouped[n, b] = grouped
+
+        def quantize_adj(n):
+            for b in range(len(bank_passes)):
+                quantize(adj_codes[n][b], adj_scales[n][b], adj_grouped[n, b])
+
+        def multiply_out(n):
+            bank = sum_banks.tile([P, H], F32, name="sums")
+            for b, gs in enumerate(bank_passes):
+                for slot, g in enumerate(gs):
+                    rows = slice(slot * P, (slot + 1) * P)
+                    nc.tensor.matmul_mx(
+                        out=bank[:],
+                        lhsT=adj_codes[n][b][:, rows].bitcast(FP8X4),
+                        lhsT_scale=adj_scales[n][b][:, rows],
+                        rhs=sup_codes[g][:].bitcast(FP8X4),
+                        rhs_scale=sup_scales[g][:],
+                        start=(g == 0),
+                        stop=(g == PASSES - 1),
+                    )
+            out_sums[n] = bank
+
+        def finish_out(n):
+            biased = work.tile([P, H], F32, name="out_biased")
+            nc.vector.tensor_tensor(out=biased[:], in0=out_sums[n][:], in1=bias_rows[:], op=ALU.add)
+            result = work.tile([P, H], F32, name="out_result")
+            nc.scalar.activation(out=result[:], in_=biased[:], func=ACT.Relu)
+            nc.sync.dma_start(out=out[n * P : (n + 1) * P, :], in_=result[:])
+
+        def quantize_x(g):
+            quantize(x_codes[g], x_scales[g], x_grouped[g])
+
+        def quantize_support(g):
+            quantize(sup_codes[g], sup_scales[g], sup_grouped[g])
+
+        for g in range(PASSES):
+            spread_scale(g)
+        group_w(nc.vector.tensor_copy, 0)
+        widen_adj(0, pieces=PASSES)
+        group_w(nc.scalar.copy, 1)
+        widen_adj(1)
+        turn_x(0)
+        group_x(0)
+        turn_adj(0)
+        group_adj(0)
+        quantize(w_codes, w_scales, w_grouped)
+        widen_adj(2)
+        quantize_x(0)
+        turn_x(1)
+        group_x(1)
+        multiply_support(0)
+        quantize_adj(0)
+        turn_adj(1)
+        group_support(0)
+        widen_adj(3)
+        quantize_x(1)
+        turn_x(2)
+        multiply_support(1)
+        group_adj(1)
+        group_x(2)
+        quantize_support(0)
+        widen_adj(4)
+        quantize_x(2)
+        quantize_adj(1)
+        group_support(1)
+        turn_adj(2)
+        multiply_support(2)
+        widen_adj(5)
+        group_adj(2)
+        group_support(2)
+        quantize_support(1)
+        turn_adj(3)
+        quantize_adj(2)
+        widen_adj(6)
+        group_adj(3)
+        turn_adj(4)
+        quantize_support(2)
+        group_adj(4)
+        quantize_adj(3)
+        turn_adj(5)
+        multiply_out(0)
+        widen_adj(7)
+        quantize_adj(4)
+        group_adj(5)
+        turn_adj(6)
+        finish_out(0)
+        multiply_out(1)
+        multiply_out(2)
+        widen_adj(8)
+        quantize_adj(5)
+        group_adj(6)
+        turn_adj(7)
+        finish_out(1)
+        finish_out(2)
+        multiply_out(3)
+        widen_adj(9)
+        quantize_adj(6)
+        group_adj(7)
+        turn_adj(8)
+        finish_out(3)
+        multiply_out(4)
+        widen_adj(10)
+        quantize_adj(7)
+        group_adj(8)
+        turn_adj(9)
+        finish_out(4)
+        multiply_out(5)
+        widen_adj(11)
+        quantize_adj(8)
+        group_adj(9)
+        turn_adj(10)
+        finish_out(5)
+        multiply_out(6)
+        quantize_adj(9)
+        group_adj(10)
+        turn_adj(11)
+        finish_out(6)
+        multiply_out(7)
+        quantize_adj(10)
+        group_adj(11)
+        finish_out(7)
+        quantize_adj(11)
+        multiply_out(8)
+        finish_out(8)
+        multiply_out(9)
+        finish_out(9)
+        multiply_out(10)
+        finish_out(10)
+        multiply_out(11)
+        finish_out(11)

@@ -38,7 +38,7 @@ def tile_gcn_pa_kernel(tc, x_init, adj1_bytes, adj1_scale, W1, b1, out):
         scale_rows = kept("scale_rows", N, F32)
         bias_rows = kept("bias_rows", H, BF16)
         ident = kept("ident", P, F32)
-        w_raw = kept("w_raw", PACK * H, BF16)
+        w_raw = [kept("w_raw%d" % half, PACK * H // 2, BF16) for half in range(2)]
         w_grouped = kept("w_grouped", H * PACK, BF16)
         w_codes = kept("w_codes", H, U32)
         w_scales = kept("w_scales", H, U8)
@@ -64,19 +64,27 @@ def tile_gcn_pa_kernel(tc, x_init, adj1_bytes, adj1_scale, W1, b1, out):
         def load_adj(n):
             nc.sync.dma_start(out=adj_fp8[n][:], in_=adj1_bytes[n * P : (n + 1) * P, :])
 
+        def load_w(half):
+            cols = slice(half * (H // 2), (half + 1) * (H // 2))
+            nc.sync.dma_start(
+                out=w_raw[half][:].rearrange("p (j h) -> p j h", j=PACK),
+                in_=W1.rearrange("(p j) h -> p j h", j=PACK)[:, :, cols],
+            )
+
         def load_x(g):
             rows = x_init[g * K_PASS : (g + 1) * K_PASS, :]
             nc.sync.dma_start(out=x_raw[g][:], in_=rows.rearrange("(m t) k -> m (t k)", t=PACK))
 
-        nc.scalar.dma_start(
+        nc.sync.dma_start(
             out=scale_cols[:].rearrange("p (g t) -> p g t", t=PACK),
             in_=adj1_scale.rearrange("o (g p t) -> p (o g) t", p=P, t=PACK),
         )
-        nc.sync.dma_start(out=w_raw[:], in_=W1.rearrange("(p j) h -> p (j h)", j=PACK))
+        load_w(0)
         load_adj(0)
+        load_w(1)
         for g in range(PASSES):
-            load_adj(g + 1)
             load_x(g)
+            load_adj(g + 1)
         for n in range(PASSES + 1, TILES):
             load_adj(n)
         nc.sync.dma_start(out=bias_rows[:], in_=b1.partition_broadcast(P))
@@ -93,12 +101,17 @@ def tile_gcn_pa_kernel(tc, x_init, adj1_bytes, adj1_scale, W1, b1, out):
 
         def group_w(copy, half):
             cols = H // 2
-            src = w_raw[:].rearrange("p (j h) -> p j h", j=PACK)[:, :, half * cols : (half + 1) * cols]
+            src = w_raw[half][:].rearrange("p (j h) -> p j h", j=PACK)
             dst = w_grouped[:, half * cols * PACK : (half + 1) * cols * PACK]
             copy(out=dst.rearrange("p (c i j) -> p c j i", i=4, j=PACK), in_=src.rearrange("p j (c i) -> p c j i", i=4))
 
         def quantize(codes, scales, grouped):
             nc.vector.quantize_mx(out=codes[:].bitcast(FP8X4), scales=scales[:], in_=grouped[:])
+
+        def quantize_w(half):
+            cols = slice(half * (H // 2), (half + 1) * (H // 2))
+            grouped = w_grouped[:, cols.start * PACK : cols.stop * PACK]
+            nc.vector.quantize_mx(out=w_codes[:, cols].bitcast(FP8X4), scales=w_scales[:, cols], in_=grouped)
 
         def turn_x(g):
             words = x_raw[g][:].bitcast(F32)
@@ -141,7 +154,7 @@ def tile_gcn_pa_kernel(tc, x_init, adj1_bytes, adj1_scale, W1, b1, out):
                 nc.scalar.copy(out=dst.rearrange("p (h t) -> p h t", t=PACK), in_=sup_sums[g, c][:].rearrange("p t h -> p h t"))
 
         def widen_adj(n, pieces=1):
-            wide = work.tile([P, N], BF16, name="adj_wide", align_bytes=64)
+            wide = work.tile([P, N], BF16, name="adj_wide", align_bytes=64, bufs=5)
             width = N // pieces
             for c in range(pieces):
                 cols = slice(c * width, (c + 1) * width)
@@ -187,12 +200,27 @@ def tile_gcn_pa_kernel(tc, x_init, adj1_bytes, adj1_scale, W1, b1, out):
                     )
             out_sums[n] = bank
 
+        def add_bias(n, cols):
+            biased = work.tile([P, cols.stop - cols.start], F32, name="out_biased", bufs=6)
+            nc.vector.tensor_tensor(out=biased[:], in0=out_sums[n][:, cols], in1=bias_rows[:, cols], op=ALU.add)
+            return biased
+
+        def result_tile(width):
+            return work.tile([P, width], F32, name="out_result", bufs=TILES + 1)
+
         def finish_out(n):
-            biased = work.tile([P, H], F32, name="out_biased")
-            nc.vector.tensor_tensor(out=biased[:], in0=out_sums[n][:], in1=bias_rows[:], op=ALU.add)
-            result = work.tile([P, H], F32, name="out_result")
+            biased = add_bias(n, slice(0, H))
+            result = result_tile(H)
             nc.scalar.activation(out=result[:], in_=biased[:], func=ACT.Relu)
             nc.sync.dma_start(out=out[n * P : (n + 1) * P, :], in_=result[:])
+
+        def finish_last(n):
+            halves = [slice(0, H // 2), slice(H // 2, H)]
+            biased = [add_bias(n, cols) for cols in halves]
+            for cols, part in zip(halves, biased):
+                result = result_tile(H // 2)
+                nc.vector.tensor_scalar_max(out=result[:], in0=part[:], scalar1=0.0)
+                nc.sync.dma_start(out=out[n * P : (n + 1) * P, cols], in_=result[:])
 
         def quantize_x(g):
             quantize(x_codes[g], x_scales[g], x_grouped[g])
@@ -203,95 +231,96 @@ def tile_gcn_pa_kernel(tc, x_init, adj1_bytes, adj1_scale, W1, b1, out):
         for g in range(PASSES):
             spread_scale(g)
         group_w(nc.vector.tensor_copy, 0)
+        quantize_w(0)
         widen_adj(0, pieces=PASSES)
         group_w(nc.scalar.copy, 1)
-        widen_adj(1)
         turn_x(0)
         group_x(0)
-        turn_adj(0)
-        group_adj(0)
-        quantize(w_codes, w_scales, w_grouped)
-        widen_adj(2)
+        widen_adj(1)
+        quantize_w(1)
         quantize_x(0)
         turn_x(1)
         group_x(1)
         multiply_support(0)
-        quantize_adj(0)
-        turn_adj(1)
-        group_support(0)
-        widen_adj(3)
+        widen_adj(2)
         quantize_x(1)
         turn_x(2)
-        multiply_support(1)
-        group_adj(1)
+        group_support(0)
         group_x(2)
+        turn_adj(0)
+        multiply_support(1)
+        group_adj(0)
+        widen_adj(3)
         quantize_support(0)
+        group_support(1)
+        turn_adj(1)
+        group_adj(1)
         widen_adj(4)
         quantize_x(2)
-        quantize_adj(1)
-        group_support(1)
-        turn_adj(2)
+        quantize_adj(0)
         multiply_support(2)
-        widen_adj(5)
-        group_adj(2)
+        turn_adj(2)
         group_support(2)
+        group_adj(2)
+        widen_adj(5)
         quantize_support(1)
+        quantize_adj(1)
         turn_adj(3)
-        quantize_adj(2)
-        widen_adj(6)
         group_adj(3)
-        turn_adj(4)
+        widen_adj(6)
         quantize_support(2)
+        quantize_adj(2)
+        turn_adj(4)
         group_adj(4)
-        quantize_adj(3)
-        turn_adj(5)
         multiply_out(0)
-        widen_adj(7)
-        quantize_adj(4)
+        turn_adj(5)
         group_adj(5)
-        turn_adj(6)
-        finish_out(0)
+        widen_adj(7)
+        quantize_adj(3)
         multiply_out(1)
-        multiply_out(2)
-        widen_adj(8)
-        quantize_adj(5)
+        turn_adj(6)
         group_adj(6)
+        finish_out(0)
+        quantize_adj(4)
+        widen_adj(8)
+        multiply_out(2)
         turn_adj(7)
-        finish_out(1)
-        finish_out(2)
-        multiply_out(3)
-        widen_adj(9)
-        quantize_adj(6)
         group_adj(7)
+        finish_out(1)
+        quantize_adj(5)
+        widen_adj(9)
+        multiply_out(3)
         turn_adj(8)
-        finish_out(3)
-        multiply_out(4)
-        widen_adj(10)
-        quantize_adj(7)
         group_adj(8)
+        finish_out(2)
+        quantize_adj(6)
+        widen_adj(10)
+        multiply_out(4)
         turn_adj(9)
-        finish_out(4)
-        multiply_out(5)
-        widen_adj(11)
-        quantize_adj(8)
         group_adj(9)
+        finish_out(3)
+        quantize_adj(7)
+        widen_adj(11)
+        multiply_out(5)
         turn_adj(10)
-        finish_out(5)
-        multiply_out(6)
-        quantize_adj(9)
         group_adj(10)
+        finish_out(4)
+        quantize_adj(8)
+        multiply_out(6)
         turn_adj(11)
-        finish_out(6)
-        multiply_out(7)
-        quantize_adj(10)
         group_adj(11)
+        finish_out(5)
+        quantize_adj(9)
+        multiply_out(7)
+        finish_out(6)
+        quantize_adj(10)
+        multiply_out(8)
         finish_out(7)
         quantize_adj(11)
-        multiply_out(8)
-        finish_out(8)
         multiply_out(9)
-        finish_out(9)
         multiply_out(10)
-        finish_out(10)
+        finish_out(8)
         multiply_out(11)
-        finish_out(11)
+        finish_out(9)
+        finish_out(10)
+        finish_last(11)

@@ -39,6 +39,9 @@ def tile_gcn_pa_kernel(tc, x_init, adj1_bytes, adj1_scale, W1, b1, out):
         bias_rows = kept("bias_rows", H, BF16)
         ident = kept("ident", P, F32)
         w_raw = [kept("w_raw%d" % half, PACK * H // 2, BF16) for half in range(2)]
+        ident_bf16 = kept("ident_bf16", P, BF16)
+        bias_cols = kept("bias_cols", H // P, F32)
+        warm_src = kept("warm_src", P, BF16)
         w_grouped = kept("w_grouped", H * PACK, BF16)
         w_codes = kept("w_codes", H, U32)
         w_scales = kept("w_scales", H, U8)
@@ -60,6 +63,9 @@ def tile_gcn_pa_kernel(tc, x_init, adj1_bytes, adj1_scale, W1, b1, out):
         x_turned = {}
         sup_sums = {}
         out_sums = {}
+        out_biased = {}
+        out_turned = {}
+        out_back = {}
 
         def load_adj(n):
             nc.sync.dma_start(out=adj_fp8[n][:], in_=adj1_bytes[n * P : (n + 1) * P, :])
@@ -90,6 +96,14 @@ def tile_gcn_pa_kernel(tc, x_init, adj1_bytes, adj1_scale, W1, b1, out):
         nc.sync.dma_start(out=bias_rows[:], in_=b1.partition_broadcast(P))
 
         make_identity(nc, ident[:])
+        make_identity(nc, ident_bf16[:])
+
+        nc.vector.memset(warm_src[:], 0.0)
+
+        def keep_warm(count):
+            bank = sum_banks.tile([P, PACK, P], F32, name="sums")
+            for i in range(count):
+                nc.tensor.matmul(bank[:, i % PACK, :], lhsT=warm_src[:], rhs=warm_src[:], start=True, stop=True)
 
         def spread_scale(g):
             bank = turn_banks.tile([P, PACK, P], F32, name="turn")
@@ -208,10 +222,12 @@ def tile_gcn_pa_kernel(tc, x_init, adj1_bytes, adj1_scale, W1, b1, out):
         def result_tile(width):
             return work.tile([P, width], F32, name="out_result", bufs=TILES + 1)
 
-        def finish_out(n):
-            biased = add_bias(n, slice(0, H))
+        def bias_out(n):
+            out_biased[n] = add_bias(n, slice(0, H))
+
+        def store_out(n):
             result = result_tile(H)
-            nc.scalar.activation(out=result[:], in_=biased[:], func=ACT.Relu)
+            nc.scalar.activation(out=result[:], in_=out_biased[n][:], func=ACT.Relu)
             nc.sync.dma_start(out=out[n * P : (n + 1) * P, :], in_=result[:])
 
         def finish_last(n):
@@ -222,14 +238,57 @@ def tile_gcn_pa_kernel(tc, x_init, adj1_bytes, adj1_scale, W1, b1, out):
                 nc.vector.tensor_scalar_max(out=result[:], in0=part[:], scalar1=0.0)
                 nc.sync.dma_start(out=out[n * P : (n + 1) * P, cols], in_=result[:])
 
+        def turn_bias():
+            bank = sum_banks.tile([P, H // P, P], BF16, name="sums")
+            for c in range(H // P):
+                nc.tensor.transpose(bank[:, c, :], bias_rows[:, c * P : (c + 1) * P], ident_bf16[:])
+            nc.scalar.copy(out=bias_cols[:].unsqueeze(2), in_=bank[:, :, 0:1])
+
+        def multiply_out_turned(n):
+            bank = sum_banks.tile([P, H // P, P], F32, name="sums")
+            for c in range(H // P):
+                cols = slice(c * P, (c + 1) * P)
+                for b, gs in enumerate(bank_passes):
+                    for slot, g in enumerate(gs):
+                        rows = slice(slot * P, (slot + 1) * P)
+                        nc.tensor.matmul_mx(
+                            out=bank[:, c, :],
+                            lhsT=sup_codes[g][:, cols].bitcast(FP8X4),
+                            lhsT_scale=sup_scales[g][:, cols],
+                            rhs=adj_codes[n][b][:, rows].bitcast(FP8X4),
+                            rhs_scale=adj_scales[n][b][:, rows],
+                            start=(g == 0),
+                            stop=(g == PASSES - 1),
+                        )
+            out_sums[n] = bank
+
+        def relu_turned(n):
+            done = work.tile([P, H // P, P], F32, name="out_turned")
+            for c in range(H // P):
+                nc.scalar.activation(out=done[:, c, :], in_=out_sums[n][:, c, :], func=ACT.Relu, bias=bias_cols[:, c : c + 1])
+            out_turned[n] = done
+
+        def turn_back(n):
+            bank = sum_banks.tile([P, H], F32, name="sums")
+            for c in range(H // P):
+                nc.tensor.transpose(bank[:, c * P : (c + 1) * P], out_turned[n][:, c, :], ident[:])
+            out_back[n] = bank
+
+        def store_turned(n):
+            result = result_tile(H)
+            nc.scalar.copy(out=result[:], in_=out_back[n][:])
+            nc.sync.dma_start(out=out[n * P : (n + 1) * P, :], in_=result[:])
+
         def quantize_x(g):
             quantize(x_codes[g], x_scales[g], x_grouped[g])
 
         def quantize_support(g):
             quantize(sup_codes[g], sup_scales[g], sup_grouped[g])
 
+        keep_warm(12)
         for g in range(PASSES):
             spread_scale(g)
+        keep_warm(12)
         group_w(nc.vector.tensor_copy, 0)
         quantize_w(0)
         widen_adj(0, pieces=PASSES)
@@ -239,6 +298,7 @@ def tile_gcn_pa_kernel(tc, x_init, adj1_bytes, adj1_scale, W1, b1, out):
         widen_adj(1)
         quantize_w(1)
         quantize_x(0)
+        keep_warm(8)
         turn_x(1)
         group_x(1)
         multiply_support(0)
@@ -265,62 +325,78 @@ def tile_gcn_pa_kernel(tc, x_init, adj1_bytes, adj1_scale, W1, b1, out):
         widen_adj(5)
         quantize_support(1)
         quantize_adj(1)
+        keep_warm(8)
         turn_adj(3)
         group_adj(3)
+        turn_bias()
         widen_adj(6)
         quantize_support(2)
         quantize_adj(2)
+        keep_warm(8)
         turn_adj(4)
         group_adj(4)
-        multiply_out(0)
-        turn_adj(5)
-        group_adj(5)
+        multiply_out_turned(0)
+        multiply_out_turned(1)
         widen_adj(7)
         quantize_adj(3)
-        multiply_out(1)
-        turn_adj(6)
-        group_adj(6)
-        finish_out(0)
-        quantize_adj(4)
-        widen_adj(8)
+        relu_turned(0)
+        relu_turned(1)
+        turn_adj(5)
+        turn_back(0)
+        turn_back(1)
+        group_adj(5)
         multiply_out(2)
-        turn_adj(7)
-        group_adj(7)
-        finish_out(1)
-        quantize_adj(5)
-        widen_adj(9)
         multiply_out(3)
-        turn_adj(8)
-        group_adj(8)
-        finish_out(2)
-        quantize_adj(6)
-        widen_adj(10)
+        widen_adj(8)
+        quantize_adj(4)
+        store_turned(0)
+        store_turned(1)
+        turn_adj(6)
+        turn_adj(7)
+        group_adj(6)
+        widen_adj(9)
+        quantize_adj(5)
+        group_adj(7)
         multiply_out(4)
-        turn_adj(9)
-        group_adj(9)
-        finish_out(3)
-        quantize_adj(7)
-        widen_adj(11)
         multiply_out(5)
-        turn_adj(10)
-        group_adj(10)
-        finish_out(4)
-        quantize_adj(8)
+        widen_adj(10)
+        quantize_adj(6)
+        bias_out(2)
+        store_out(2)
+        turn_adj(8)
+        turn_adj(9)
+        group_adj(8)
+        widen_adj(11)
+        quantize_adj(7)
+        bias_out(3)
+        group_adj(9)
+        store_out(3)
+        bias_out(4)
+        store_out(4)
         multiply_out(6)
+        turn_adj(10)
         turn_adj(11)
-        group_adj(11)
-        finish_out(5)
+        quantize_adj(8)
+        bias_out(5)
+        group_adj(10)
+        store_out(5)
         quantize_adj(9)
+        group_adj(11)
         multiply_out(7)
-        finish_out(6)
-        quantize_adj(10)
         multiply_out(8)
-        finish_out(7)
-        quantize_adj(11)
         multiply_out(9)
+        bias_out(6)
+        store_out(6)
+        quantize_adj(10)
+        bias_out(7)
+        store_out(7)
+        quantize_adj(11)
         multiply_out(10)
-        finish_out(8)
         multiply_out(11)
-        finish_out(9)
-        finish_out(10)
+        bias_out(8)
+        store_out(8)
+        bias_out(9)
+        store_out(9)
+        bias_out(10)
+        store_out(10)
         finish_last(11)

from contextlib import ExitStack

import concourse.mybir as mybir
from concourse.masks import make_identity

N, F, H = 1536, 512, 512
FLOPS = 2 * N * F * H + 2 * N * N * H

F32 = mybir.dt.float32
BF16 = mybir.dt.bfloat16
U32 = mybir.dt.uint32
U8 = mybir.dt.uint8
FP8 = mybir.dt.float8_e4m3fn
FP8X4 = mybir.dt.float8_e4m3fn_x4
ALU = mybir.AluOpType
ACT = mybir.ActivationFunctionType

P = 128
PACK = 4
K_PASS = P * PACK
PASSES = N // K_PASS
TILES = N // P


def tile_gcn_pa_kernel(tc, x_init, adj1_bytes, adj1_scale, W1, b1, out):
    nc = tc.nc
    with ExitStack() as ctx:
        keep = ctx.enter_context(tc.tile_pool(name="keep", bufs=1))
        work = ctx.enter_context(tc.tile_pool(name="work", bufs=4))
        turn_banks = ctx.enter_context(tc.psum_pool(name="turn_banks", bufs=4))
        sum_banks = ctx.enter_context(tc.psum_pool(name="sum_banks", bufs=4))
        ctx.enter_context(tc.manual_schedule())

        def kept(name, width, dtype):
            return keep.tile([P, width], dtype, name=name, align_bytes=64)

        scale_cols = kept("scale_cols", PASSES * PACK, F32)
        scale_rows = kept("scale_rows", N, F32)
        bias_rows = kept("bias_rows", H, BF16)
        ident = kept("ident", P, F32)
        w_raw = [kept("w_raw%d" % half, PACK * H // 2, BF16) for half in range(2)]
        ident_bf16 = kept("ident_bf16", P, BF16)
        bias_cols = kept("bias_cols", H // P, F32)
        warm_src = kept("warm_src", P, BF16)
        w_grouped = kept("w_grouped", H * PACK, BF16)
        w_codes = kept("w_codes", H, U32)
        w_scales = kept("w_scales", H, U8)
        x_raw = [kept("x_raw%d" % g, PACK * F, BF16) for g in range(PASSES)]
        x_grouped = [kept("x_grouped%d" % g, K_PASS * PACK, BF16) for g in range(PASSES)]
        x_codes = [kept("x_codes%d" % g, K_PASS, U32) for g in range(PASSES)]
        x_scales = [kept("x_scales%d" % g, K_PASS, U8) for g in range(PASSES)]
        sup_grouped = [kept("sup_grouped%d" % g, H * PACK, BF16) for g in range(PASSES)]
        sup_codes = [kept("sup_codes%d" % g, H, U32) for g in range(PASSES)]
        sup_scales = [kept("sup_scales%d" % g, H, U8) for g in range(PASSES)]
        adj_fp8 = [kept("adj_fp8_%d" % n, N, U8) for n in range(TILES)]
        bank_passes = [(0, 1), (2,)]
        adj_codes = [[kept("adj_codes%d_%d" % (n, b), P * len(gs), U32) for b, gs in enumerate(bank_passes)] for n in range(TILES)]
        adj_scales = [[kept("adj_scales%d_%d" % (n, b), P * len(gs), U8) for b, gs in enumerate(bank_passes)] for n in range(TILES)]

        adj_wide = {}
        adj_turned = {}
        adj_grouped = {}
        x_turned = {}
        sup_sums = {}
        out_sums = {}
        out_biased = {}
        out_turned = {}
        out_back = {}

        def load_adj(n):
            nc.sync.dma_start(out=adj_fp8[n][:], in_=adj1_bytes[n * P : (n + 1) * P, :])

        def load_w(half):
            cols = slice(half * (H // 2), (half + 1) * (H // 2))
            nc.sync.dma_start(
                out=w_raw[half][:].rearrange("p (j h) -> p j h", j=PACK),
                in_=W1.rearrange("(p j) h -> p j h", j=PACK)[:, :, cols],
            )

        def load_x(g):
            rows = x_init[g * K_PASS : (g + 1) * K_PASS, :]
            nc.sync.dma_start(out=x_raw[g][:], in_=rows.rearrange("(m t) k -> m (t k)", t=PACK))

        nc.sync.dma_start(
            out=scale_cols[:].rearrange("p (g t) -> p g t", t=PACK),
            in_=adj1_scale.rearrange("o (g p t) -> p (o g) t", p=P, t=PACK),
        )
        load_w(0)
        load_adj(0)
        load_w(1)
        for g in range(PASSES):
            load_x(g)
            load_adj(g + 1)
        for n in range(PASSES + 1, TILES):
            load_adj(n)
        nc.sync.dma_start(out=bias_rows[:], in_=b1.partition_broadcast(P))

        make_identity(nc, ident[:])
        make_identity(nc, ident_bf16[:])

        nc.vector.memset(warm_src[:], 0.0)

        def keep_warm(count):
            bank = sum_banks.tile([P, PACK, P], F32, name="sums")
            for i in range(count):
                nc.tensor.matmul(bank[:, i % PACK, :], lhsT=warm_src[:], rhs=warm_src[:], start=True, stop=True)

        def spread_scale(g):
            bank = turn_banks.tile([P, PACK, P], F32, name="turn")
            for t in range(PACK):
                col = g * PACK + t
                nc.tensor.transpose(bank[:, t, :], scale_cols[:, col : col + 1].to_broadcast([P, P]), ident[:])
            rows = scale_rows[:, g * K_PASS : (g + 1) * K_PASS]
            nc.scalar.copy(out=rows.rearrange("q (p t) -> q p t", t=PACK), in_=bank[:].rearrange("q t p -> q p t"))

        def group_w(copy, half):
            cols = H // 2
            src = w_raw[half][:].rearrange("p (j h) -> p j h", j=PACK)
            dst = w_grouped[:, half * cols * PACK : (half + 1) * cols * PACK]
            copy(out=dst.rearrange("p (c i j) -> p c j i", i=4, j=PACK), in_=src.rearrange("p j (c i) -> p c j i", i=4))

        def quantize(codes, scales, grouped):
            nc.vector.quantize_mx(out=codes[:].bitcast(FP8X4), scales=scales[:], in_=grouped[:])

        def quantize_w(half):
            cols = slice(half * (H // 2), (half + 1) * (H // 2))
            grouped = w_grouped[:, cols.start * PACK : cols.stop * PACK]
            nc.vector.quantize_mx(out=w_codes[:, cols].bitcast(FP8X4), scales=w_scales[:, cols], in_=grouped)

        def turn_x(g):
            words = x_raw[g][:].bitcast(F32)
            for b in range(2):
                bank = turn_banks.tile([P, 2, 2, P], F32, name="turn")
                for tt in range(2):
                    first = (2 * b + tt) * (F // 2)
                    for u in range(2):
                        nc.tensor.transpose(bank[:, tt, u, :], words[:, first + u : first + F // 2 : 2], ident[:])
                x_turned[g, b] = bank

        def group_x(g):
            for b in range(2):
                dst = x_grouped[g][:, b * 2 * K_PASS : (b + 1) * 2 * K_PASS].bitcast(F32)
                nc.scalar.copy(
                    out=dst.rearrange("p (t m u) -> p t m u", t=2, u=2),
                    in_=x_turned[g, b][:].rearrange("p t u m -> p t m u"),
                )

        def multiply_support(g):
            for c in range(H // P):
                bank = sum_banks.tile([P, PACK, P], F32, name="sums")
                cols = slice(c * P, (c + 1) * P)
                for t in range(PACK):
                    nodes = slice(t * P, (t + 1) * P)
                    nc.tensor.matmul_mx(
                        out=bank[:, t, :],
                        lhsT=x_codes[g][:, nodes].bitcast(FP8X4),
                        lhsT_scale=x_scales[g][:, nodes],
                        rhs=w_codes[:, cols].bitcast(FP8X4),
                        rhs_scale=w_scales[:, cols],
                        start=True,
                        stop=True,
                    )
                sup_sums[g, c] = bank

        def group_support(g):
            for c in range(H // P):
                dst = sup_grouped[g][:, c * K_PASS : (c + 1) * K_PASS]
                nc.scalar.copy(out=dst.rearrange("p (h t) -> p h t", t=PACK), in_=sup_sums[g, c][:].rearrange("p t h -> p h t"))

        def widen_adj(n, pieces=1):
            wide = work.tile([P, N], BF16, name="adj_wide", align_bytes=64, bufs=5)
            width = N // pieces
            for c in range(pieces):
                cols = slice(c * width, (c + 1) * width)
                nc.vector.tensor_tensor(out=wide[:, cols], in0=adj_fp8[n][:, cols].bitcast(FP8), in1=scale_rows[:, cols], op=ALU.mult)
            adj_wide[n] = wide

        def turn_adj(n):
            words = adj_wide[n][:].bitcast(F32)
            for b, gs in enumerate(bank_passes):
                bank = turn_banks.tile([P, len(gs), 2, P], F32, name="turn")
                for slot, g in enumerate(gs):
                    first = g * (K_PASS // 2)
                    for u in range(2):
                        nc.tensor.transpose(bank[:, slot, u, :], words[:, first + u : first + K_PASS // 2 : 2], ident[:])
                adj_turned[n, b] = bank

        def group_adj(n):
            for b, gs in enumerate(bank_passes):
                grouped = work.tile([P, len(gs) * K_PASS], BF16, name="adj_grouped%d" % b, align_bytes=64)
                nc.scalar.copy(
                    out=grouped[:].bitcast(F32).rearrange("p (g r u) -> p g r u", g=len(gs), u=2),
                    in_=adj_turned[n, b][:].rearrange("p g u r -> p g r u"),
                )
                adj_grouped[n, b] = grouped

        def quantize_adj(n):
            for b in range(len(bank_passes)):
                quantize(adj_codes[n][b], adj_scales[n][b], adj_grouped[n, b])

        def multiply_out(n):
            bank = sum_banks.tile([P, H], F32, name="sums")
            for b, gs in enumerate(bank_passes):
                for slot, g in enumerate(gs):
                    rows = slice(slot * P, (slot + 1) * P)
                    nc.tensor.matmul_mx(
                        out=bank[:],
                        lhsT=adj_codes[n][b][:, rows].bitcast(FP8X4),
                        lhsT_scale=adj_scales[n][b][:, rows],
                        rhs=sup_codes[g][:].bitcast(FP8X4),
                        rhs_scale=sup_scales[g][:],
                        start=(g == 0),
                        stop=(g == PASSES - 1),
                    )
            out_sums[n] = bank

        def add_bias(n, cols):
            biased = work.tile([P, cols.stop - cols.start], F32, name="out_biased", bufs=6)
            nc.vector.tensor_tensor(out=biased[:], in0=out_sums[n][:, cols], in1=bias_rows[:, cols], op=ALU.add)
            return biased

        def result_tile(width):
            return work.tile([P, width], F32, name="out_result", bufs=TILES + 1)

        def bias_out(n):
            out_biased[n] = add_bias(n, slice(0, H))

        def store_out(n):
            result = result_tile(H)
            nc.scalar.activation(out=result[:], in_=out_biased[n][:], func=ACT.Relu)
            nc.sync.dma_start(out=out[n * P : (n + 1) * P, :], in_=result[:])

        def finish_last(n):
            halves = [slice(0, H // 2), slice(H // 2, H)]
            biased = [add_bias(n, cols) for cols in halves]
            for cols, part in zip(halves, biased):
                result = result_tile(H // 2)
                nc.vector.tensor_scalar_max(out=result[:], in0=part[:], scalar1=0.0)
                nc.sync.dma_start(out=out[n * P : (n + 1) * P, cols], in_=result[:])

        def turn_bias():
            bank = sum_banks.tile([P, H // P, P], BF16, name="sums")
            for c in range(H // P):
                nc.tensor.transpose(bank[:, c, :], bias_rows[:, c * P : (c + 1) * P], ident_bf16[:])
            nc.scalar.copy(out=bias_cols[:].unsqueeze(2), in_=bank[:, :, 0:1])

        def multiply_out_turned(n):
            bank = sum_banks.tile([P, H // P, P], F32, name="sums")
            for c in range(H // P):
                cols = slice(c * P, (c + 1) * P)
                for b, gs in enumerate(bank_passes):
                    for slot, g in enumerate(gs):
                        rows = slice(slot * P, (slot + 1) * P)
                        nc.tensor.matmul_mx(
                            out=bank[:, c, :],
                            lhsT=sup_codes[g][:, cols].bitcast(FP8X4),
                            lhsT_scale=sup_scales[g][:, cols],
                            rhs=adj_codes[n][b][:, rows].bitcast(FP8X4),
                            rhs_scale=adj_scales[n][b][:, rows],
                            start=(g == 0),
                            stop=(g == PASSES - 1),
                        )
            out_sums[n] = bank

        def relu_turned(n):
            done = work.tile([P, H // P, P], F32, name="out_turned")
            for c in range(H // P):
                nc.scalar.activation(out=done[:, c, :], in_=out_sums[n][:, c, :], func=ACT.Relu, bias=bias_cols[:, c : c + 1])
            out_turned[n] = done

        def turn_back(n):
            bank = sum_banks.tile([P, H], F32, name="sums")
            for c in range(H // P):
                nc.tensor.transpose(bank[:, c * P : (c + 1) * P], out_turned[n][:, c, :], ident[:])
            out_back[n] = bank

        def store_turned(n):
            result = result_tile(H)
            nc.scalar.copy(out=result[:], in_=out_back[n][:])
            nc.sync.dma_start(out=out[n * P : (n + 1) * P, :], in_=result[:])

        def quantize_x(g):
            quantize(x_codes[g], x_scales[g], x_grouped[g])

        def quantize_support(g):
            quantize(sup_codes[g], sup_scales[g], sup_grouped[g])

        keep_warm(12)
        for g in range(PASSES):
            spread_scale(g)
        keep_warm(12)
        group_w(nc.vector.tensor_copy, 0)
        quantize_w(0)
        widen_adj(0, pieces=PASSES)
        group_w(nc.scalar.copy, 1)
        turn_x(0)
        group_x(0)
        widen_adj(1)
        quantize_w(1)
        quantize_x(0)
        keep_warm(8)
        turn_x(1)
        group_x(1)
        multiply_support(0)
        widen_adj(2)
        quantize_x(1)
        turn_x(2)
        group_support(0)
        group_x(2)
        turn_adj(0)
        multiply_support(1)
        group_adj(0)
        widen_adj(3)
        quantize_support(0)
        group_support(1)
        turn_adj(1)
        group_adj(1)
        widen_adj(4)
        quantize_x(2)
        quantize_adj(0)
        multiply_support(2)
        turn_adj(2)
        group_support(2)
        group_adj(2)
        widen_adj(5)
        quantize_support(1)
        quantize_adj(1)
        keep_warm(8)
        turn_adj(3)
        group_adj(3)
        turn_bias()
        widen_adj(6)
        quantize_support(2)
        quantize_adj(2)
        keep_warm(8)
        turn_adj(4)
        group_adj(4)
        multiply_out_turned(0)
        multiply_out_turned(1)
        widen_adj(7)
        quantize_adj(3)
        relu_turned(0)
        relu_turned(1)
        turn_adj(5)
        turn_back(0)
        turn_back(1)
        group_adj(5)
        multiply_out(2)
        multiply_out(3)
        widen_adj(8)
        quantize_adj(4)
        store_turned(0)
        store_turned(1)
        turn_adj(6)
        turn_adj(7)
        group_adj(6)
        widen_adj(9)
        quantize_adj(5)
        group_adj(7)
        multiply_out(4)
        multiply_out(5)
        widen_adj(10)
        quantize_adj(6)
        bias_out(2)
        store_out(2)
        turn_adj(8)
        turn_adj(9)
        group_adj(8)
        widen_adj(11)
        quantize_adj(7)
        bias_out(3)
        group_adj(9)
        store_out(3)
        bias_out(4)
        store_out(4)
        multiply_out(6)
        turn_adj(10)
        turn_adj(11)
        quantize_adj(8)
        bias_out(5)
        group_adj(10)
        store_out(5)
        quantize_adj(9)
        group_adj(11)
        multiply_out(7)
        multiply_out(8)
        multiply_out(9)
        bias_out(6)
        store_out(6)
        quantize_adj(10)
        bias_out(7)
        store_out(7)
        quantize_adj(11)
        multiply_out(10)
        multiply_out(11)
        bias_out(8)
        store_out(8)
        bias_out(9)
        store_out(9)
        bias_out(10)
        store_out(10)
        finish_last(11)
